import numpy as np
import ml_dtypes


def mxq(x, axis, fmt="e4m3"):
    dtype, down = {"e4m3": (ml_dtypes.float8_e4m3fn, 7), "e5m2": (ml_dtypes.float8_e5m2, 14)}[fmt]
    v = np.moveaxis(np.asarray(x, np.float32).astype(ml_dtypes.bfloat16).astype(np.float64), axis, -1)
    blocks = v.reshape(v.shape[:-1] + (-1, 32))
    amax = np.abs(blocks).max(-1, keepdims=True)
    byte = np.maximum(np.where(amax > 0, np.frexp(amax)[1] - 1 + 127, 0) - down, 1)
    scale = np.exp2(byte - 127.0)
    codes = (blocks / scale).astype(np.float32).astype(dtype).astype(np.float64)
    return np.moveaxis((codes * scale).reshape(v.shape), -1, axis)


WIDE = False


def mx_kscale(k):
    if not WIDE:
        return np.ones(k)
    levels = np.array([10, -10, 5, -5, 0])
    a = np.random.permutation(np.resize(levels, k // 512 * 4)).reshape(k // 512, 4)
    idx = np.arange(k)
    return np.exp2(a[idx // 512, idx % 128 // 32])


BF16 = ml_dtypes.bfloat16


def bf(x):
    return np.asarray(x, np.float32).astype(BF16)


def f64(x):
    return np.asarray(x).astype(np.float64)


N, C, H, W = 4, 1024, 32, 32

REPARAM_OFFSET = 2.0 ** -18
PEDESTAL = REPARAM_OFFSET ** 2
BETA_MIN = 1e-6
BOUND_BETA = (BETA_MIN + PEDESTAL) ** 0.5
BOUND_GAMMA = PEDESTAL ** 0.5
INVERSE = False


def nn_reparam(v, bound):
    return np.square(np.maximum(v, bound)) - PEDESTAL


def setup_inputs():
    u = np.exp2(np.round(np.log2(mx_kscale(C)) / 2))
    amp = np.exp(0.5 * np.random.standard_normal((N, 1, H, W)))
    x = np.random.standard_normal((N, C, H, W)) * amp * u[None, :, None, None]
    beta = np.random.standard_normal(C) * u
    gamma = np.random.standard_normal((C, C)) * 1.5 / np.sqrt(C) * u[:, None] / u[None, :]
    return {"x": bf(x), "beta": bf(beta), "gamma": bf(gamma)}


def reference(x, beta, gamma):
    x = f64(x)
    beta_eff = nn_reparam(f64(beta), BOUND_BETA)
    gamma_eff = nn_reparam(f64(gamma), BOUND_GAMMA)
    x2 = x * x
    denom_sq = (mxq(gamma_eff, 1, "e4m3") @ mxq(x2, 1, "e4m3").reshape(N, C, H * W)).reshape(N, C, H, W)
    denom_sq = denom_sq + beta_eff[None, :, None, None]
    norm = np.sqrt(denom_sq) if INVERSE else 1.0 / np.sqrt(denom_sq)
    return x * norm

@@ -1,0 +1,181 @@
+from contextlib import ExitStack
+
+import concourse.mybir as mybir
+from concourse.masks import make_identity
+
+F32 = mybir.dt.float32
+BF16 = mybir.dt.bfloat16
+U32 = mybir.dt.uint32
+U8 = mybir.dt.uint8
+FP8X4 = mybir.dt.float8_e4m3fn_x4
+ALU = mybir.AluOpType
+ACT = mybir.ActivationFunctionType
+
+P = 128
+NIMG = 4
+C = 1024
+HW = 1024
+FLOPS = 2 * NIMG * C * C * HW
+
+PEDESTAL = 2.0 ** -36
+BOUND_BETA = (1e-6 + PEDESTAL) ** 0.5
+
+WS = 288
+LEAD = 4
+
+
+def tile_einsumgdn_t_kernel(tc, x, beta, gamma, out):
+    nc = tc.nc
+    x_v = x.rearrange("n (g s p e) h w -> n g p s (e h w)", g=2, s=2, p=P, e=2)
+    out_v = out.rearrange("n (t p e) h w -> n t p (e h w)", t=4, p=P, e=2)
+    gamma_v = gamma.rearrange("(t p e) c -> t p (e c)", t=4, p=P, e=2)
+    beta_v = beta.rearrange("(t p e) -> p t e", t=4, p=P, e=2)
+
+    with ExitStack() as ctx:
+        const = ctx.enter_context(tc.tile_pool(name="const", bufs=1))
+        xpool = ctx.enter_context(tc.tile_pool(name="xpool", bufs=1))
+        gpool = ctx.enter_context(tc.tile_pool(name="gpool", bufs=2))
+        work = ctx.enter_context(tc.tile_pool(name="work", bufs=3))
+        opool = ctx.enter_context(tc.tile_pool(name="opool", bufs=6))
+        psum = ctx.enter_context(tc.psum_pool(name="psum", bufs=8))
+
+        warm = const.tile([P, 1], F32, name="warm")
+        warm2 = const.tile([P, 1], F32, name="warm2")
+        nc.vector.memset(warm[:], 1.0)
+        nc.scalar.activation(out=warm2[:], in_=warm[:], func=ACT.Abs_reciprocal_sqrt)
+
+        ident = const.tile([P, P], F32, name="ident")
+        make_identity(nc, ident[:])
+
+        graw = []
+        for t in range(4):
+            gt = gpool.tile([P, 2 * C], BF16, name="graw", bufs=4)
+            nc.sync.dma_start(out=gt[:], in_=gamma_v[t])
+            graw.append(gt)
+        bt = const.tile([P, 4, 2], BF16, name="bt")
+        with nc.allow_non_contiguous_dma(reason="beta: one pair of channels a partition"):
+            nc.scalar.dma_start(out=bt[:], in_=beta_v)
+        xs = {}
+        for n in range(NIMG):
+            for g in range(2):
+                xt = xpool.tile([P, 4, HW], BF16, name="xs%d%d" % (n, g))
+                nc.sync.dma_start(
+                    out=xt[:].rearrange("p (s e) w -> p s (e w)", s=2), in_=x_v[n, g]
+                )
+                xs[(n, g)] = xt
+
+        bmax = const.tile([P, 8], F32, name="bmax")
+        beff = const.tile([P, 8], F32, name="beff")
+        nc.vector.tensor_scalar(
+            out=bmax[:], in0=bt[:].rearrange("p t e -> p (t e)"),
+            scalar1=BOUND_BETA, scalar2=None, op0=ALU.max,
+        )
+        nc.vector.tensor_tensor(out=beff[:], in0=bmax[:], in1=bmax[:], op=ALU.mult)
+        nc.vector.tensor_scalar(
+            out=beff[:], in0=beff[:], scalar1=-PEDESTAL, scalar2=None, op0=ALU.add
+        )
+
+        gcodes = const.tile([P, 4, 512], U32, name="gcodes", align_bytes=64)
+        gsc = const.tile([P, 4, 512], U8, name="gsc", align_bytes=64)
+        for t in range(4):
+            grelu = gpool.tile([P, 2 * C], BF16, name="grelu")
+            nc.vector.tensor_scalar(
+                out=grelu[:], in0=graw[t][:], scalar1=0.0, scalar2=None, op0=ALU.max
+            )
+            gw = grelu[:].bitcast(F32)
+            gg = gpool.tile([P, 2, 1024], BF16, name="gg", align_bytes=64)
+            for g in range(2):
+                bank = psum.tile([P, 512], F32, name="bank")
+                for u in range(2):
+                    for e1 in range(2):
+                        src0 = 512 * e1 + 256 * g + 128 * u
+                        dst0 = 256 * u + 128 * e1
+                        nc.tensor.transpose(
+                            bank[:, dst0 : dst0 + 128], gw[:, src0 : src0 + 128], ident[:]
+                        )
+                sq = work.tile([P, 1024], F32, name="sq")
+                nc.scalar.activation(
+                    out=sq[:].rearrange("p (j u e) -> p j u e", u=2, e=2),
+                    in_=bank[:].bitcast(BF16).rearrange("p (u j e) -> p j u e", u=2, e=2),
+                    func=ACT.Square,
+                )
+                nc.vector.tensor_scalar(
+                    out=gg[:, g, :], in0=sq[:], scalar1=-PEDESTAL, scalar2=0.0,
+                    op0=ALU.add, op1=ALU.max,
+                )
+            nc.vector.quantize_mx(
+                out=gcodes[:, t, :].bitcast(FP8X4),
+                scales=gsc[:, t, :],
+                in_=gg[:].rearrange("p g k -> p (g k)"),
+            )
+
+        xcodes = {}
+        xsc = {}
+
+        def piece(k):
+            n, g, half = k // 4, (k // 2) % 2, k % 2
+            if (k % 4) == 0:
+                xcodes[n] = work.tile([P, 2, HW], U32, name="xcodes", align_bytes=64)
+                xsc[n] = work.tile([P, 2, HW], U8, name="xsc", align_bytes=64)
+            grp = work.tile([P, 512, 4], BF16, name="grp", bufs=4, align_bytes=64)
+            w0 = 512 * half
+            src = xs[(n, g)]
+            nc.scalar.activation(
+                out=grp[:, 0:WS, :].rearrange("p (c i) t -> p c t i", i=4),
+                in_=src[:, :, w0 : w0 + WS].rearrange("p t (c i) -> p c t i", i=4),
+                func=ACT.Square,
+            )
+            vsrc = src[:, :, w0 + WS : w0 + 512].rearrange("p t (c i) -> p c t i", i=4)
+            nc.vector.tensor_tensor(
+                out=grp[:, WS:512, :].rearrange("p (c i) t -> p c t i", i=4),
+                in0=vsrc, in1=vsrc, op=ALU.mult,
+            )
+            nc.vector.quantize_mx(
+                out=xcodes[n][:, g, w0 : w0 + 512].bitcast(FP8X4),
+                scales=xsc[n][:, g, w0 : w0 + 512],
+                in_=grp[:].rearrange("p w t -> p (w t)"),
+            )
+
+        def slot(k):
+            n, t = k // 4, k % 4
+            o = opool.tile([P, 2, HW], F32, name="o")
+            for e1 in range(2):
+                banks = []
+                for h in range(2):
+                    acc = psum.tile([P, 512], F32, name="bank")
+                    banks.append(acc)
+                for g in range(2):
+                    m0 = 256 * g + 128 * e1
+                    for h in range(2):
+                        nc.tensor.matmul_mx(
+                            out=banks[h][:],
+                            lhsT=gcodes[:, t, m0 : m0 + 128].bitcast(FP8X4),
+                            lhsT_scale=gsc[:, t, m0 : m0 + 128],
+                            rhs=xcodes[n][:, g, 512 * h : 512 * h + 512].bitcast(FP8X4),
+                            rhs_scale=xsc[n][:, g, 512 * h : 512 * h + 512],
+                            start=(g == 0),
+                            stop=(g == 1),
+                        )
+                for h in range(2):
+                    nc.scalar.activation(
+                        out=o[:, e1, 512 * h : 512 * h + 512],
+                        in_=banks[h][:],
+                        func=ACT.Abs_reciprocal_sqrt,
+                        bias=beff[:, 2 * t + e1 : 2 * t + e1 + 1],
+                        scale=1.0,
+                    )
+            o2 = o[:].rearrange("p e w -> p (e w)")
+            r0 = 2 * (t % 2)
+            nc.vector.tensor_tensor(
+                out=o2, in0=o2,
+                in1=xs[(n, t // 2)][:, r0 : r0 + 2, :].rearrange("p e w -> p (e w)"),
+                op=ALU.mult,
+            )
+            nc.sync.dma_start(out=out_v[n, t], in_=o2)
+
+        for k in range(LEAD):
+            piece(k)
+        for k in range(16):
+            if k + LEAD < 16:
+                piece(k + LEAD)
+            slot(k)

@@ -20,8 +20,10 @@ FLOPS = 2 * NIMG * C * C * HW
 PEDESTAL = 2.0 ** -36
 BOUND_BETA = (1e-6 + PEDESTAL) ** 0.5
 
-WS = 288
-LEAD = 4
+WS = 312
+LEAD = 6
+NPIECE = 16
+NSLOT = 16
 
 
 def tile_einsumgdn_t_kernel(tc, x, beta, gamma, out):
@@ -36,8 +38,27 @@ def tile_einsumgdn_t_kernel(tc, x, beta, gamma, out):
         xpool = ctx.enter_context(tc.tile_pool(name="xpool", bufs=1))
         gpool = ctx.enter_context(tc.tile_pool(name="gpool", bufs=2))
         work = ctx.enter_context(tc.tile_pool(name="work", bufs=3))
-        opool = ctx.enter_context(tc.tile_pool(name="opool", bufs=6))
+        opool = ctx.enter_context(tc.tile_pool(name="opool", bufs=5))
         psum = ctx.enter_context(tc.psum_pool(name="psum", bufs=8))
+        ctx.enter_context(tc.manual_schedule())
+
+        graw = []
+        for t in range(4):
+            gt = gpool.tile([P, 2 * C], BF16, name="graw", bufs=4)
+            nc.sync.dma_start(out=gt[:], in_=gamma_v[t])
+            graw.append(gt)
+        xs = {}
+        bt = const.tile([P, 4, 2], BF16, name="bt")
+        for n in range(NIMG):
+            for g in range(2):
+                xt = xpool.tile([P, 4, HW], BF16, name="xs%d%d" % (n, g))
+                nc.sync.dma_start(
+                    out=xt[:].rearrange("p (s e) w -> p s (e w)", s=2), in_=x_v[n, g]
+                )
+                xs[(n, g)] = xt
+            if n == 0:
+                with nc.allow_non_contiguous_dma(reason="beta: one pair of channels a partition"):
+                    nc.sync.dma_start(out=bt[:], in_=beta_v)
 
         warm = const.tile([P, 1], F32, name="warm")
         warm2 = const.tile([P, 1], F32, name="warm2")
@@ -47,22 +68,158 @@ def tile_einsumgdn_t_kernel(tc, x, beta, gamma, out):
         ident = const.tile([P, P], F32, name="ident")
         make_identity(nc, ident[:])
 
-        graw = []
-        for t in range(4):
-            gt = gpool.tile([P, 2 * C], BF16, name="graw", bufs=4)
-            nc.sync.dma_start(out=gt[:], in_=gamma_v[t])
-            graw.append(gt)
-        bt = const.tile([P, 4, 2], BF16, name="bt")
-        with nc.allow_non_contiguous_dma(reason="beta: one pair of channels a partition"):
-            nc.scalar.dma_start(out=bt[:], in_=beta_v)
-        xs = {}
-        for n in range(NIMG):
+        gcodes = const.tile([P, 4, 512], U32, name="gcodes", align_bytes=64)
+        gsc = const.tile([P, 4, 512], U8, name="gsc", align_bytes=64)
+        grelu = {}
+        gbank = {}
+        gsq = {}
+        gg = {}
+
+        def g_relu(t):
+            grelu[t] = gpool.tile([P, 2 * C], BF16, name="grelu", bufs=3)
+            nc.vector.tensor_scalar(
+                out=grelu[t][:], in0=graw[t][:], scalar1=0.0, scalar2=None, op0=ALU.max
+            )
+
+        def g_transpose(t):
+            gw = grelu[t][:].bitcast(F32)
             for g in range(2):
-                xt = xpool.tile([P, 4, HW], BF16, name="xs%d%d" % (n, g))
-                nc.sync.dma_start(
-                    out=xt[:].rearrange("p (s e) w -> p s (e w)", s=2), in_=x_v[n, g]
+                bank = psum.tile([P, 512], F32, name="bank")
+                for u in range(2):
+                    for e1 in range(2):
+                        src0 = 512 * e1 + 256 * g + 128 * u
+                        dst0 = 256 * u + 128 * e1
+                        nc.tensor.transpose(
+                            bank[:, dst0 : dst0 + 128], gw[:, src0 : src0 + 128], ident[:]
+                        )
+                gbank[(t, g)] = bank
+
+        def g_square(t, g):
+            sq = work.tile([P, 1024], F32, name="sq", bufs=4)
+            nc.scalar.activation(
+                out=sq[:].rearrange("p (j u e) -> p j u e", u=2, e=2),
+                in_=gbank[(t, g)][:].bitcast(BF16).rearrange("p (u j e) -> p j u e", u=2, e=2),
+                func=ACT.Square,
+            )
+            gsq[(t, g)] = sq
+
+        def g_sub(t, g):
+            if g == 0:
+                gg[t] = gpool.tile([P, 2, 1024], BF16, name="gg", bufs=3, align_bytes=64)
+            nc.vector.tensor_scalar(
+                out=gg[t][:, g, :], in0=gsq[(t, g)][:], scalar1=-PEDESTAL, scalar2=0.0,
+                op0=ALU.add, op1=ALU.max,
+            )
+
+        def g_quant(t):
+            nc.vector.quantize_mx(
+                out=gcodes[:, t, :].bitcast(FP8X4),
+                scales=gsc[:, t, :],
+                in_=gg[t][:].rearrange("p g k -> p (g k)"),
+            )
+
+        xcodes = {}
+        xsc = {}
+        grp = {}
+
+        def where(j):
+            return j // 4, (j // 2) % 2, 512 * (j % 2)
+
+        def sq_alloc(j):
+            n = j // 4
+            if (j % 4) == 0:
+                xcodes[n] = work.tile([P, 2, HW], U32, name="xcodes", align_bytes=64)
+                xsc[n] = work.tile([P, 2, HW], U8, name="xsc", align_bytes=64)
+            grp[j] = work.tile([P, 512, 4], BF16, name="grp", bufs=4, align_bytes=64)
+
+        def sq_scalar(j):
+            n, g, w0 = where(j)
+            nc.scalar.activation(
+                out=grp[j][:, 0:WS, :].rearrange("p (c i) t -> p c t i", i=4),
+                in_=xs[(n, g)][:, :, w0 : w0 + WS].rearrange("p t (c i) -> p c t i", i=4),
+                func=ACT.Square,
+            )
+
+        def sq_vector(j):
+            n, g, w0 = where(j)
+            vsrc = xs[(n, g)][:, :, w0 + WS : w0 + 512].rearrange("p t (c i) -> p c t i", i=4)
+            nc.vector.tensor_tensor(
+                out=grp[j][:, WS:512, :].rearrange("p (c i) t -> p c t i", i=4),
+                in0=vsrc, in1=vsrc, op=ALU.mult,
+            )
+
+        def sq_quant(j):
+            n, g, w0 = where(j)
+            nc.vector.quantize_mx(
+                out=xcodes[n][:, g, w0 : w0 + 512].bitcast(FP8X4),
+                scales=xsc[n][:, g, w0 : w0 + 512],
+                in_=grp[j][:].rearrange("p w t -> p (w t)"),
+            )
+
+        acc = {}
+        otile = {}
+
+        def mm(k):
+            n, t = k // 4, k % 4
+            for e1 in range(2):
+                for h in range(2):
+                    bank = psum.tile([P, 512], F32, name="bank")
+                    acc[(k, e1, h)] = bank
+                    for g in range(2):
+                        m0 = 256 * g + 128 * e1
+                        nc.tensor.matmul_mx(
+                            out=bank[:],
+                            lhsT=gcodes[:, t, m0 : m0 + 128].bitcast(FP8X4),
+                            lhsT_scale=gsc[:, t, m0 : m0 + 128],
+                            rhs=xcodes[n][:, g, 512 * h : 512 * h + 512].bitcast(FP8X4),
+                            rhs_scale=xsc[n][:, g, 512 * h : 512 * h + 512],
+                            start=(g == 0),
+                            stop=(g == 1),
+                        )
+
+        def rsq(k):
+            t = k % 4
+            otile[k] = opool.tile([P, 2 * HW], F32, name="o")
+            for e1 in range(2):
+                for h in range(2):
+                    c0 = HW * e1 + 512 * h
+                    nc.scalar.activation(
+                        out=otile[k][:, c0 : c0 + 512],
+                        in_=acc[(k, e1, h)][:],
+                        func=ACT.Abs_reciprocal_sqrt,
+                        bias=beff[:, 2 * t + e1 : 2 * t + e1 + 1],
+                        scale=1.0,
+                    )
+
+        def finish(k, parts):
+            n, t = k // 4, k % 4
+            xrow = xs[(n, t // 2)][:, 2 * (t % 2) : 2 * (t % 2) + 2, :].rearrange("p e w -> p (e w)")
+            width = 2 * HW // parts
+            for q in range(parts):
+                cols = slice(q * width, (q + 1) * width)
+                nc.vector.tensor_tensor(
+                    out=otile[k][:, cols], in0=otile[k][:, cols], in1=xrow[:, cols], op=ALU.mult
                 )
-                xs[(n, g)] = xt
+                nc.sync.dma_start(out=out_v[n, t][:, cols], in_=otile[k][:, cols])
+
+        g_relu(0)
+        g_transpose(0)
+        g_relu(1)
+        g_transpose(1)
+        early = 0
+        for t in range(4):
+            g_square(t, 0)
+            g_square(t, 1)
+            if t + 2 < 4:
+                g_relu(t + 2)
+                g_transpose(t + 2)
+            g_sub(t, 0)
+            g_sub(t, 1)
+            if t >= 1:
+                g_quant(t - 1)
+                sq_alloc(early)
+                sq_vector(early)
+                early += 1
 
         bmax = const.tile([P, 8], F32, name="bmax")
         beff = const.tile([P, 8], F32, name="beff")
@@ -74,108 +231,28 @@ def tile_einsumgdn_t_kernel(tc, x, beta, gamma, out):
         nc.vector.tensor_scalar(
             out=beff[:], in0=beff[:], scalar1=-PEDESTAL, scalar2=None, op0=ALU.add
         )
+        g_quant(3)
 
-        gcodes = const.tile([P, 4, 512], U32, name="gcodes", align_bytes=64)
-        gsc = const.tile([P, 4, 512], U8, name="gsc", align_bytes=64)
-        for t in range(4):
-            grelu = gpool.tile([P, 2 * C], BF16, name="grelu")
-            nc.vector.tensor_scalar(
-                out=grelu[:], in0=graw[t][:], scalar1=0.0, scalar2=None, op0=ALU.max
-            )
-            gw = grelu[:].bitcast(F32)
-            gg = gpool.tile([P, 2, 1024], BF16, name="gg", align_bytes=64)
-            for g in range(2):
-                bank = psum.tile([P, 512], F32, name="bank")
-                for u in range(2):
-                    for e1 in range(2):
-                        src0 = 512 * e1 + 256 * g + 128 * u
-                        dst0 = 256 * u + 128 * e1
-                        nc.tensor.transpose(
-                            bank[:, dst0 : dst0 + 128], gw[:, src0 : src0 + 128], ident[:]
-                        )
-                sq = work.tile([P, 1024], F32, name="sq")
-                nc.scalar.activation(
-                    out=sq[:].rearrange("p (j u e) -> p j u e", u=2, e=2),
-                    in_=bank[:].bitcast(BF16).rearrange("p (u j e) -> p j u e", u=2, e=2),
-                    func=ACT.Square,
-                )
-                nc.vector.tensor_scalar(
-                    out=gg[:, g, :], in0=sq[:], scalar1=-PEDESTAL, scalar2=0.0,
-                    op0=ALU.add, op1=ALU.max,
-                )
-            nc.vector.quantize_mx(
-                out=gcodes[:, t, :].bitcast(FP8X4),
-                scales=gsc[:, t, :],
-                in_=gg[:].rearrange("p g k -> p (g k)"),
-            )
+        for j in range(LEAD):
+            if j >= early:
+                sq_alloc(j)
+                sq_vector(j)
+            sq_scalar(j)
+            if j >= 1:
+                sq_quant(j - 1)
+        pending = LEAD - 1
 
-        xcodes = {}
-        xsc = {}
-
-        def piece(k):
-            n, g, half = k // 4, (k // 2) % 2, k % 2
-            if (k % 4) == 0:
-                xcodes[n] = work.tile([P, 2, HW], U32, name="xcodes", align_bytes=64)
-                xsc[n] = work.tile([P, 2, HW], U8, name="xsc", align_bytes=64)
-            grp = work.tile([P, 512, 4], BF16, name="grp", bufs=4, align_bytes=64)
-            w0 = 512 * half
-            src = xs[(n, g)]
-            nc.scalar.activation(
-                out=grp[:, 0:WS, :].rearrange("p (c i) t -> p c t i", i=4),
-                in_=src[:, :, w0 : w0 + WS].rearrange("p t (c i) -> p c t i", i=4),
-                func=ACT.Square,
-            )
-            vsrc = src[:, :, w0 + WS : w0 + 512].rearrange("p t (c i) -> p c t i", i=4)
-            nc.vector.tensor_tensor(
-                out=grp[:, WS:512, :].rearrange("p (c i) t -> p c t i", i=4),
-                in0=vsrc, in1=vsrc, op=ALU.mult,
-            )
-            nc.vector.quantize_mx(
-                out=xcodes[n][:, g, w0 : w0 + 512].bitcast(FP8X4),
-                scales=xsc[n][:, g, w0 : w0 + 512],
-                in_=grp[:].rearrange("p w t -> p (w t)"),
-            )
-
-        def slot(k):
-            n, t = k // 4, k % 4
-            o = opool.tile([P, 2, HW], F32, name="o")
-            for e1 in range(2):
-                banks = []
-                for h in range(2):
-                    acc = psum.tile([P, 512], F32, name="bank")
-                    banks.append(acc)
-                for g in range(2):
-                    m0 = 256 * g + 128 * e1
-                    for h in range(2):
-                        nc.tensor.matmul_mx(
-                            out=banks[h][:],
-                            lhsT=gcodes[:, t, m0 : m0 + 128].bitcast(FP8X4),
-                            lhsT_scale=gsc[:, t, m0 : m0 + 128],
-                            rhs=xcodes[n][:, g, 512 * h : 512 * h + 512].bitcast(FP8X4),
-                            rhs_scale=xsc[n][:, g, 512 * h : 512 * h + 512],
-                            start=(g == 0),
-                            stop=(g == 1),
-                        )
-                for h in range(2):
-                    nc.scalar.activation(
-                        out=o[:, e1, 512 * h : 512 * h + 512],
-                        in_=banks[h][:],
-                        func=ACT.Abs_reciprocal_sqrt,
-                        bias=beff[:, 2 * t + e1 : 2 * t + e1 + 1],
-                        scale=1.0,
-                    )
-            o2 = o[:].rearrange("p e w -> p (e w)")
-            r0 = 2 * (t % 2)
-            nc.vector.tensor_tensor(
-                out=o2, in0=o2,
-                in1=xs[(n, t // 2)][:, r0 : r0 + 2, :].rearrange("p e w -> p (e w)"),
-                op=ALU.mult,
-            )
-            nc.sync.dma_start(out=out_v[n, t], in_=o2)
-
-        for k in range(LEAD):
-            piece(k)
-        for k in range(16):
-            if k + LEAD < 16:
-                piece(k + LEAD)
-            slot(k)
+        for k in range(NSLOT):
+            j = k + LEAD
+            if j < NPIECE:
+                sq_alloc(j)
+                sq_scalar(j)
+                sq_vector(j)
+            mm(k)
+            rsq(k)
+            if k >= 1:
+                finish(k - 1, 2 if k - 1 == NSLOT - 2 else 1)
+            if pending < NPIECE:
+                sq_quant(pending)
+                pending += 1
+        finish(NSLOT - 1, 4)

@@ -20,18 +20,26 @@ FLOPS = 2 * NIMG * C * C * HW
 PEDESTAL = 2.0 ** -36
 BOUND_BETA = (1e-6 + PEDESTAL) ** 0.5
 
-WS = 312
-LEAD = 6
-NPIECE = 16
+WS = 304
+WS_LAST = 360
+LEAD = 7
+HALVES_FROM = 9
 NSLOT = 16
 
 
 def tile_einsumgdn_t_kernel(tc, x, beta, gamma, out):
     nc = tc.nc
     x_v = x.rearrange("n (g s p e) h w -> n g p s (e h w)", g=2, s=2, p=P, e=2)
+    x_c = x.rearrange("n (g s p e) h w -> n g s p e (h w)", g=2, s=2, p=P, e=2)
     out_v = out.rearrange("n (t p e) h w -> n t p (e h w)", t=4, p=P, e=2)
-    gamma_v = gamma.rearrange("(t p e) c -> t p (e c)", t=4, p=P, e=2)
+    gamma_v = gamma.rearrange("(t p e) c -> t p e c", t=4, p=P, e=2)
     beta_v = beta.rearrange("(t p e) -> p t e", t=4, p=P, e=2)
+
+    pieces = [(0, 0, 0, 256, 256), (0, 0, 256, 256, 0), (0, 0, 512, 512, WS)]
+    for j in range(2, 16):
+        pieces.append((j // 4, (j // 2) % 2, 512 * (j % 2), 512, WS if j < 14 else WS_LAST))
+    npiece = len(pieces)
+    first_parts = [(0, 256), (256, 256), (512, 512)]
 
     with ExitStack() as ctx:
         const = ctx.enter_context(tc.tile_pool(name="const", bufs=1))
@@ -42,20 +50,41 @@ def tile_einsumgdn_t_kernel(tc, x, beta, gamma, out):
         psum = ctx.enter_context(tc.psum_pool(name="psum", bufs=8))
         ctx.enter_context(tc.manual_schedule())
 
-        graw = []
-        for t in range(4):
-            gt = gpool.tile([P, 2 * C], BF16, name="graw", bufs=4)
-            nc.sync.dma_start(out=gt[:], in_=gamma_v[t])
-            graw.append(gt)
+        graw = {}
+        for g in range(2):
+            graw[(0, g)] = gpool.tile([P, 2, 512], BF16, name="graw0%d" % g, bufs=1)
+        for t in range(1, 4):
+            graw[t] = gpool.tile([P, 2, C], BF16, name="graw", bufs=3)
         xs = {}
-        bt = const.tile([P, 4, 2], BF16, name="bt")
+        xfirst = []
+        for q in range(3):
+            xfirst.append(xpool.tile([P, 4, first_parts[q][1]], BF16, name="xfirst%d" % q))
         for n in range(NIMG):
             for g in range(2):
-                xt = xpool.tile([P, 4, HW], BF16, name="xs%d%d" % (n, g))
+                if (n, g) != (0, 0):
+                    xs[(n, g)] = xpool.tile([P, 4, HW], BF16, name="xs%d%d" % (n, g))
+        bt = const.tile([P, 4, 2], BF16, name="bt")
+
+        def load_first(q):
+            w0, wd = first_parts[q]
+            for s in range(2):
                 nc.sync.dma_start(
-                    out=xt[:].rearrange("p (s e) w -> p s (e w)", s=2), in_=x_v[n, g]
+                    out=xfirst[q][:, 2 * s : 2 * s + 2, :], in_=x_c[0, 0, s][:, :, w0 : w0 + wd]
                 )
-                xs[(n, g)] = xt
+
+        nc.sync.dma_start(out=graw[(0, 0)][:], in_=gamma_v[0][:, :, 0:512])
+        load_first(0)
+        nc.sync.dma_start(out=graw[(0, 1)][:], in_=gamma_v[0][:, :, 512:1024])
+        load_first(1)
+        load_first(2)
+        for t in range(1, 4):
+            nc.sync.dma_start(out=graw[t][:], in_=gamma_v[t])
+        for n in range(NIMG):
+            for g in range(2):
+                if (n, g) != (0, 0):
+                    nc.sync.dma_start(
+                        out=xs[(n, g)][:].rearrange("p (s e) w -> p s (e w)", s=2), in_=x_v[n, g]
+                    )
             if n == 0:
                 with nc.allow_non_contiguous_dma(reason="beta: one pair of channels a partition"):
                     nc.sync.dma_start(out=bt[:], in_=beta_v)
@@ -75,24 +104,27 @@ def tile_einsumgdn_t_kernel(tc, x, beta, gamma, out):
         gsq = {}
         gg = {}
 
-        def g_relu(t):
-            grelu[t] = gpool.tile([P, 2 * C], BF16, name="grelu", bufs=3)
+        def g_relu(key):
+            if key in (1, 2, 3):
+                grelu[key] = gpool.tile([P, 2, C], BF16, name="grelu", bufs=3)
+            else:
+                grelu[key] = gpool.tile([P, 2, 512], BF16, name="grelu0%d" % key[1], bufs=1)
             nc.vector.tensor_scalar(
-                out=grelu[t][:], in0=graw[t][:], scalar1=0.0, scalar2=None, op0=ALU.max
+                out=grelu[key][:], in0=graw[key][:], scalar1=0.0, scalar2=None, op0=ALU.max
             )
 
-        def g_transpose(t):
-            gw = grelu[t][:].bitcast(F32)
-            for g in range(2):
-                bank = psum.tile([P, 512], F32, name="bank")
-                for u in range(2):
-                    for e1 in range(2):
-                        src0 = 512 * e1 + 256 * g + 128 * u
-                        dst0 = 256 * u + 128 * e1
-                        nc.tensor.transpose(
-                            bank[:, dst0 : dst0 + 128], gw[:, src0 : src0 + 128], ident[:]
-                        )
-                gbank[(t, g)] = bank
+        def g_transpose(t, g):
+            src = grelu[(0, g)] if t == 0 else grelu[t]
+            gw = src[:].rearrange("p e c -> p (e c)").bitcast(F32)
+            bank = psum.tile([P, 512], F32, name="bank")
+            for u in range(2):
+                for e1 in range(2):
+                    src0 = (256 * e1 + 128 * u) if t == 0 else (512 * e1 + 256 * g + 128 * u)
+                    dst0 = 256 * u + 128 * e1
+                    nc.tensor.transpose(
+                        bank[:, dst0 : dst0 + 128], gw[:, src0 : src0 + 128], ident[:]
+                    )
+            gbank[(t, g)] = bank
 
         def g_square(t, g):
             sq = work.tile([P, 1024], F32, name="sq", bufs=4)
@@ -122,38 +154,44 @@ def tile_einsumgdn_t_kernel(tc, x, beta, gamma, out):
         xsc = {}
         grp = {}
 
-        def where(j):
-            return j // 4, (j // 2) % 2, 512 * (j % 2)
+        def sq_tile(j):
+            if j not in grp:
+                grp[j] = work.tile([P, 512, 4], BF16, name="grp", bufs=4, align_bytes=64)
+            return grp[j]
 
-        def sq_alloc(j):
-            n = j // 4
-            if (j % 4) == 0:
-                xcodes[n] = work.tile([P, 2, HW], U32, name="xcodes", align_bytes=64)
-                xsc[n] = work.tile([P, 2, HW], U8, name="xsc", align_bytes=64)
-            grp[j] = work.tile([P, 512, 4], BF16, name="grp", bufs=4, align_bytes=64)
+        def sq_source(j, c0, c1):
+            n, g, w0, wd, ws = pieces[j]
+            if j < 3:
+                return xfirst[j][:, :, c0:c1]
+            return xs[(n, g)][:, :, w0 + c0 : w0 + c1]
 
         def sq_scalar(j):
-            n, g, w0 = where(j)
-            nc.scalar.activation(
-                out=grp[j][:, 0:WS, :].rearrange("p (c i) t -> p c t i", i=4),
-                in_=xs[(n, g)][:, :, w0 : w0 + WS].rearrange("p t (c i) -> p c t i", i=4),
-                func=ACT.Square,
-            )
+            n, g, w0, wd, ws = pieces[j]
+            if ws > 0:
+                nc.scalar.activation(
+                    out=sq_tile(j)[:, 0:ws, :].rearrange("p (c i) t -> p c t i", i=4),
+                    in_=sq_source(j, 0, ws).rearrange("p t (c i) -> p c t i", i=4),
+                    func=ACT.Square,
+                )
 
         def sq_vector(j):
-            n, g, w0 = where(j)
-            vsrc = xs[(n, g)][:, :, w0 + WS : w0 + 512].rearrange("p t (c i) -> p c t i", i=4)
-            nc.vector.tensor_tensor(
-                out=grp[j][:, WS:512, :].rearrange("p (c i) t -> p c t i", i=4),
-                in0=vsrc, in1=vsrc, op=ALU.mult,
-            )
+            n, g, w0, wd, ws = pieces[j]
+            if ws < wd:
+                vsrc = sq_source(j, ws, wd).rearrange("p t (c i) -> p c t i", i=4)
+                nc.vector.tensor_tensor(
+                    out=sq_tile(j)[:, ws:wd, :].rearrange("p (c i) t -> p c t i", i=4),
+                    in0=vsrc, in1=vsrc, op=ALU.mult,
+                )
 
         def sq_quant(j):
-            n, g, w0 = where(j)
+            n, g, w0, wd, ws = pieces[j]
+            if n not in xcodes:
+                xcodes[n] = work.tile([P, 2, HW], U32, name="xcodes", align_bytes=64)
+                xsc[n] = work.tile([P, 2, HW], U8, name="xsc", align_bytes=64)
             nc.vector.quantize_mx(
-                out=xcodes[n][:, g, w0 : w0 + 512].bitcast(FP8X4),
-                scales=xsc[n][:, g, w0 : w0 + 512],
-                in_=grp[j][:].rearrange("p w t -> p (w t)"),
+                out=xcodes[n][:, g, w0 : w0 + wd].bitcast(FP8X4),
+                scales=xsc[n][:, g, w0 : w0 + wd],
+                in_=grp[j][:, 0:wd, :].rearrange("p w t -> p (w t)"),
             )
 
         acc = {}
@@ -191,35 +229,69 @@ def tile_einsumgdn_t_kernel(tc, x, beta, gamma, out):
                         scale=1.0,
                     )
 
-        def finish(k, parts):
+        def finish(k, b0, b1):
             n, t = k // 4, k % 4
-            xrow = xs[(n, t // 2)][:, 2 * (t % 2) : 2 * (t % 2) + 2, :].rearrange("p e w -> p (e w)")
-            width = 2 * HW // parts
-            for q in range(parts):
-                cols = slice(q * width, (q + 1) * width)
+            r0 = 2 * (t % 2)
+            cols = slice(512 * b0, 512 * b1)
+            if (n, t // 2) == (0, 0):
+                o3 = otile[k][:].rearrange("p (e w) -> p e w", e=2)
+                for q in range(3):
+                    w0, wd = first_parts[q]
+                    nc.vector.tensor_tensor(
+                        out=o3[:, :, w0 : w0 + wd], in0=o3[:, :, w0 : w0 + wd],
+                        in1=xfirst[q][:, r0 : r0 + 2, :], op=ALU.mult,
+                    )
+            else:
+                xrow = xs[(n, t // 2)][:, r0 : r0 + 2, :].rearrange("p e w -> p (e w)")
                 nc.vector.tensor_tensor(
                     out=otile[k][:, cols], in0=otile[k][:, cols], in1=xrow[:, cols], op=ALU.mult
                 )
-                nc.sync.dma_start(out=out_v[n, t][:, cols], in_=otile[k][:, cols])
+            nc.sync.dma_start(out=out_v[n, t][:, cols], in_=otile[k][:, cols])
 
-        g_relu(0)
-        g_transpose(0)
+        g_relu((0, 0))
+        g_transpose(0, 0)
+        sq_scalar(0)
+        g_relu((0, 1))
+        g_transpose(0, 1)
+        g_square(0, 0)
+        g_square(0, 1)
+        sq_quant(0)
+        sq_vector(1)
+        sq_vector(2)
+        sq_scalar(2)
         g_relu(1)
-        g_transpose(1)
-        early = 0
-        for t in range(4):
-            g_square(t, 0)
-            g_square(t, 1)
-            if t + 2 < 4:
-                g_relu(t + 2)
-                g_transpose(t + 2)
-            g_sub(t, 0)
-            g_sub(t, 1)
-            if t >= 1:
-                g_quant(t - 1)
-                sq_alloc(early)
-                sq_vector(early)
-                early += 1
+        g_transpose(1, 0)
+        g_transpose(1, 1)
+        g_sub(0, 0)
+        g_relu(2)
+        g_transpose(2, 0)
+        g_transpose(2, 1)
+        g_sub(0, 1)
+        g_square(1, 0)
+        g_square(1, 1)
+        g_relu(3)
+        g_transpose(3, 0)
+        g_transpose(3, 1)
+        sq_quant(1)
+        g_quant(0)
+        sq_quant(2)
+        g_sub(1, 0)
+        g_sub(1, 1)
+        g_square(2, 0)
+        g_square(2, 1)
+        sq_vector(3)
+        g_quant(1)
+        g_sub(2, 0)
+        g_sub(2, 1)
+        g_square(3, 0)
+        g_square(3, 1)
+        sq_vector(4)
+        g_quant(2)
+        sq_scalar(3)
+        sq_scalar(4)
+        g_sub(3, 0)
+        g_sub(3, 1)
+        sq_quant(3)
 
         bmax = const.tile([P, 8], F32, name="bmax")
         beff = const.tile([P, 8], F32, name="beff")
@@ -232,27 +304,34 @@ def tile_einsumgdn_t_kernel(tc, x, beta, gamma, out):
             out=beff[:], in0=beff[:], scalar1=-PEDESTAL, scalar2=None, op0=ALU.add
         )
         g_quant(3)
+        sq_quant(4)
 
-        for j in range(LEAD):
-            if j >= early:
-                sq_alloc(j)
-                sq_vector(j)
+        vnext = 5
+        qnext = 5
+        for j in range(5, LEAD):
             sq_scalar(j)
-            if j >= 1:
-                sq_quant(j - 1)
-        pending = LEAD - 1
+            while vnext <= j + 1:
+                sq_vector(vnext)
+                vnext += 1
+            if qnext < j:
+                sq_quant(qnext)
+                qnext += 1
 
         for k in range(NSLOT):
             j = k + LEAD
-            if j < NPIECE:
-                sq_alloc(j)
+            if j < npiece:
                 sq_scalar(j)
-                sq_vector(j)
             mm(k)
             rsq(k)
             if k >= 1:
-                finish(k - 1, 2 if k - 1 == NSLOT - 2 else 1)
-            if pending < NPIECE:
-                sq_quant(pending)
-                pending += 1
-        finish(NSLOT - 1, 4)
+                finish(k - 1, 2 if k - 1 >= HALVES_FROM else 0, 4)
+            while vnext <= j + 1 and vnext < npiece:
+                sq_vector(vnext)
+                vnext += 1
+            if qnext < npiece:
+                sq_quant(qnext)
+                qnext += 1
+            if HALVES_FROM <= k < NSLOT - 1:
+                finish(k, 0, 2)
+        for b in range(4):
+            finish(NSLOT - 1, b, b + 1)

@@ -20,8 +20,8 @@ FLOPS = 2 * NIMG * C * C * HW
 PEDESTAL = 2.0 ** -36
 BOUND_BETA = (1e-6 + PEDESTAL) ** 0.5
 
-WS = 304
-WS_LAST = 360
+WS = 328
+WS_LAST = 384
 LEAD = 7
 HALVES_FROM = 9
 NSLOT = 16

@@ -20,8 +20,8 @@ FLOPS = 2 * NIMG * C * C * HW
 PEDESTAL = 2.0 ** -36
 BOUND_BETA = (1e-6 + PEDESTAL) ** 0.5
 
-WS = 328
-WS_LAST = 384
+WS = 280
+WS_LAST = 336
 LEAD = 7
 HALVES_FROM = 9
 NSLOT = 16

@@ -20,8 +20,8 @@ FLOPS = 2 * NIMG * C * C * HW
 PEDESTAL = 2.0 ** -36
 BOUND_BETA = (1e-6 + PEDESTAL) ** 0.5
 
-WS = 280
-WS_LAST = 336
+WS = 308
+WS_LAST = 364
 LEAD = 7
 HALVES_FROM = 9
 NSLOT = 16
@@ -76,8 +76,9 @@ def tile_einsumgdn_t_kernel(tc, x, beta, gamma, out):
         load_first(0)
         nc.sync.dma_start(out=graw[(0, 1)][:], in_=gamma_v[0][:, :, 512:1024])
         load_first(1)
+        nc.sync.dma_start(out=graw[1][:], in_=gamma_v[1])
         load_first(2)
-        for t in range(1, 4):
+        for t in range(2, 4):
             nc.sync.dma_start(out=graw[t][:], in_=gamma_v[t])
         for n in range(NIMG):
             for g in range(2):
@@ -221,18 +222,21 @@ def tile_einsumgdn_t_kernel(tc, x, beta, gamma, out):
             for e1 in range(2):
                 for h in range(2):
                     c0 = HW * e1 + 512 * h
-                    nc.scalar.activation(
-                        out=otile[k][:, c0 : c0 + 512],
-                        in_=acc[(k, e1, h)][:],
-                        func=ACT.Abs_reciprocal_sqrt,
-                        bias=beff[:, 2 * t + e1 : 2 * t + e1 + 1],
-                        scale=1.0,
-                    )
+                    cuts = 2 if (k, e1, h) == (NSLOT - 1, 1, 1) else 1
+                    wd = 512 // cuts
+                    for q in range(cuts):
+                        nc.scalar.activation(
+                            out=otile[k][:, c0 + q * wd : c0 + (q + 1) * wd],
+                            in_=acc[(k, e1, h)][:, q * wd : (q + 1) * wd],
+                            func=ACT.Abs_reciprocal_sqrt,
+                            bias=beff[:, 2 * t + e1 : 2 * t + e1 + 1],
+                            scale=1.0,
+                        )
 
-        def finish(k, b0, b1):
+        def finish(k, c0, c1):
             n, t = k // 4, k % 4
             r0 = 2 * (t % 2)
-            cols = slice(512 * b0, 512 * b1)
+            cols = slice(c0, c1)
             if (n, t // 2) == (0, 0):
                 o3 = otile[k][:].rearrange("p (e w) -> p e w", e=2)
                 for q in range(3):
@@ -257,11 +261,11 @@ def tile_einsumgdn_t_kernel(tc, x, beta, gamma, out):
         g_square(0, 1)
         sq_quant(0)
         sq_vector(1)
-        sq_vector(2)
-        sq_scalar(2)
         g_relu(1)
         g_transpose(1, 0)
         g_transpose(1, 1)
+        sq_vector(2)
+        sq_scalar(2)
         g_sub(0, 0)
         g_relu(2)
         g_transpose(2, 0)
@@ -324,7 +328,7 @@ def tile_einsumgdn_t_kernel(tc, x, beta, gamma, out):
             mm(k)
             rsq(k)
             if k >= 1:
-                finish(k - 1, 2 if k - 1 >= HALVES_FROM else 0, 4)
+                finish(k - 1, HW if k - 1 >= HALVES_FROM else 0, 2 * HW)
             while vnext <= j + 1 and vnext < npiece:
                 sq_vector(vnext)
                 vnext += 1
@@ -332,6 +336,6 @@ def tile_einsumgdn_t_kernel(tc, x, beta, gamma, out):
                 sq_quant(qnext)
                 qnext += 1
             if HALVES_FROM <= k < NSLOT - 1:
-                finish(k, 0, 2)
-        for b in range(4):
-            finish(NSLOT - 1, b, b + 1)
+                finish(k, 0, HW)
+        for c0, c1 in ((0, 512), (512, 1024), (1024, 1536), (1536, 1792), (1792, 2048)):
+            finish(NSLOT - 1, c0, c1)

from contextlib import ExitStack

import concourse.mybir as mybir
from concourse.masks import make_identity

F32 = mybir.dt.float32
BF16 = mybir.dt.bfloat16
U32 = mybir.dt.uint32
U8 = mybir.dt.uint8
FP8X4 = mybir.dt.float8_e4m3fn_x4
ALU = mybir.AluOpType
ACT = mybir.ActivationFunctionType

P = 128
NIMG = 4
C = 1024
HW = 1024
FLOPS = 2 * NIMG * C * C * HW

PEDESTAL = 2.0 ** -36
BOUND_BETA = (1e-6 + PEDESTAL) ** 0.5

WS = 308
WS_LAST = 364
LEAD = 7
HALVES_FROM = 9
NSLOT = 16


def tile_einsumgdn_t_kernel(tc, x, beta, gamma, out):
    nc = tc.nc
    x_v = x.rearrange("n (g s p e) h w -> n g p s (e h w)", g=2, s=2, p=P, e=2)
    x_c = x.rearrange("n (g s p e) h w -> n g s p e (h w)", g=2, s=2, p=P, e=2)
    out_v = out.rearrange("n (t p e) h w -> n t p (e h w)", t=4, p=P, e=2)
    gamma_v = gamma.rearrange("(t p e) c -> t p e c", t=4, p=P, e=2)
    beta_v = beta.rearrange("(t p e) -> p t e", t=4, p=P, e=2)

    pieces = [(0, 0, 0, 256, 256), (0, 0, 256, 256, 0), (0, 0, 512, 512, WS)]
    for j in range(2, 16):
        pieces.append((j // 4, (j // 2) % 2, 512 * (j % 2), 512, WS if j < 14 else WS_LAST))
    npiece = len(pieces)
    first_parts = [(0, 256), (256, 256), (512, 512)]

    with ExitStack() as ctx:
        const = ctx.enter_context(tc.tile_pool(name="const", bufs=1))
        xpool = ctx.enter_context(tc.tile_pool(name="xpool", bufs=1))
        gpool = ctx.enter_context(tc.tile_pool(name="gpool", bufs=2))
        work = ctx.enter_context(tc.tile_pool(name="work", bufs=3))
        opool = ctx.enter_context(tc.tile_pool(name="opool", bufs=5))
        psum = ctx.enter_context(tc.psum_pool(name="psum", bufs=8))
        ctx.enter_context(tc.manual_schedule())

        graw = {}
        for g in range(2):
            graw[(0, g)] = gpool.tile([P, 2, 512], BF16, name="graw0%d" % g, bufs=1)
        for t in range(1, 4):
            graw[t] = gpool.tile([P, 2, C], BF16, name="graw", bufs=3)
        xs = {}
        xfirst = []
        for q in range(3):
            xfirst.append(xpool.tile([P, 4, first_parts[q][1]], BF16, name="xfirst%d" % q))
        for n in range(NIMG):
            for g in range(2):
                if (n, g) != (0, 0):
                    xs[(n, g)] = xpool.tile([P, 4, HW], BF16, name="xs%d%d" % (n, g))
        bt = const.tile([P, 4, 2], BF16, name="bt")

        def load_first(q):
            w0, wd = first_parts[q]
            for s in range(2):
                nc.sync.dma_start(
                    out=xfirst[q][:, 2 * s : 2 * s + 2, :], in_=x_c[0, 0, s][:, :, w0 : w0 + wd]
                )

        nc.sync.dma_start(out=graw[(0, 0)][:], in_=gamma_v[0][:, :, 0:512])
        load_first(0)
        nc.sync.dma_start(out=graw[(0, 1)][:], in_=gamma_v[0][:, :, 512:1024])
        load_first(1)
        nc.sync.dma_start(out=graw[1][:], in_=gamma_v[1])
        load_first(2)
        for t in range(2, 4):
            nc.sync.dma_start(out=graw[t][:], in_=gamma_v[t])
        for n in range(NIMG):
            for g in range(2):
                if (n, g) != (0, 0):
                    nc.sync.dma_start(
                        out=xs[(n, g)][:].rearrange("p (s e) w -> p s (e w)", s=2), in_=x_v[n, g]
                    )
            if n == 0:
                with nc.allow_non_contiguous_dma(reason="beta: one pair of channels a partition"):
                    nc.sync.dma_start(out=bt[:], in_=beta_v)

        warm = const.tile([P, 1], F32, name="warm")
        warm2 = const.tile([P, 1], F32, name="warm2")
        nc.vector.memset(warm[:], 1.0)
        nc.scalar.activation(out=warm2[:], in_=warm[:], func=ACT.Abs_reciprocal_sqrt)

        ident = const.tile([P, P], F32, name="ident")
        make_identity(nc, ident[:])

        gcodes = const.tile([P, 4, 512], U32, name="gcodes", align_bytes=64)
        gsc = const.tile([P, 4, 512], U8, name="gsc", align_bytes=64)
        grelu = {}
        gbank = {}
        gsq = {}
        gg = {}

        def g_relu(key):
            if key in (1, 2, 3):
                grelu[key] = gpool.tile([P, 2, C], BF16, name="grelu", bufs=3)
            else:
                grelu[key] = gpool.tile([P, 2, 512], BF16, name="grelu0%d" % key[1], bufs=1)
            nc.vector.tensor_scalar(
                out=grelu[key][:], in0=graw[key][:], scalar1=0.0, scalar2=None, op0=ALU.max
            )

        def g_transpose(t, g):
            src = grelu[(0, g)] if t == 0 else grelu[t]
            gw = src[:].rearrange("p e c -> p (e c)").bitcast(F32)
            bank = psum.tile([P, 512], F32, name="bank")
            for u in range(2):
                for e1 in range(2):
                    src0 = (256 * e1 + 128 * u) if t == 0 else (512 * e1 + 256 * g + 128 * u)
                    dst0 = 256 * u + 128 * e1
                    nc.tensor.transpose(
                        bank[:, dst0 : dst0 + 128], gw[:, src0 : src0 + 128], ident[:]
                    )
            gbank[(t, g)] = bank

        def g_square(t, g):
            sq = work.tile([P, 1024], F32, name="sq", bufs=4)
            nc.scalar.activation(
                out=sq[:].rearrange("p (j u e) -> p j u e", u=2, e=2),
                in_=gbank[(t, g)][:].bitcast(BF16).rearrange("p (u j e) -> p j u e", u=2, e=2),
                func=ACT.Square,
            )
            gsq[(t, g)] = sq

        def g_sub(t, g):
            if g == 0:
                gg[t] = gpool.tile([P, 2, 1024], BF16, name="gg", bufs=3, align_bytes=64)
            nc.vector.tensor_scalar(
                out=gg[t][:, g, :], in0=gsq[(t, g)][:], scalar1=-PEDESTAL, scalar2=0.0,
                op0=ALU.add, op1=ALU.max,
            )

        def g_quant(t):
            nc.vector.quantize_mx(
                out=gcodes[:, t, :].bitcast(FP8X4),
                scales=gsc[:, t, :],
                in_=gg[t][:].rearrange("p g k -> p (g k)"),
            )

        xcodes = {}
        xsc = {}
        grp = {}

        def sq_tile(j):
            if j not in grp:
                grp[j] = work.tile([P, 512, 4], BF16, name="grp", bufs=4, align_bytes=64)
            return grp[j]

        def sq_source(j, c0, c1):
            n, g, w0, wd, ws = pieces[j]
            if j < 3:
                return xfirst[j][:, :, c0:c1]
            return xs[(n, g)][:, :, w0 + c0 : w0 + c1]

        def sq_scalar(j):
            n, g, w0, wd, ws = pieces[j]
            if ws > 0:
                nc.scalar.activation(
                    out=sq_tile(j)[:, 0:ws, :].rearrange("p (c i) t -> p c t i", i=4),
                    in_=sq_source(j, 0, ws).rearrange("p t (c i) -> p c t i", i=4),
                    func=ACT.Square,
                )

        def sq_vector(j):
            n, g, w0, wd, ws = pieces[j]
            if ws < wd:
                vsrc = sq_source(j, ws, wd).rearrange("p t (c i) -> p c t i", i=4)
                nc.vector.tensor_tensor(
                    out=sq_tile(j)[:, ws:wd, :].rearrange("p (c i) t -> p c t i", i=4),
                    in0=vsrc, in1=vsrc, op=ALU.mult,
                )

        def sq_quant(j):
            n, g, w0, wd, ws = pieces[j]
            if n not in xcodes:
                xcodes[n] = work.tile([P, 2, HW], U32, name="xcodes", align_bytes=64)
                xsc[n] = work.tile([P, 2, HW], U8, name="xsc", align_bytes=64)
            nc.vector.quantize_mx(
                out=xcodes[n][:, g, w0 : w0 + wd].bitcast(FP8X4),
                scales=xsc[n][:, g, w0 : w0 + wd],
                in_=grp[j][:, 0:wd, :].rearrange("p w t -> p (w t)"),
            )

        acc = {}
        otile = {}

        def mm(k):
            n, t = k // 4, k % 4
            for e1 in range(2):
                for h in range(2):
                    bank = psum.tile([P, 512], F32, name="bank")
                    acc[(k, e1, h)] = bank
                    for g in range(2):
                        m0 = 256 * g + 128 * e1
                        nc.tensor.matmul_mx(
                            out=bank[:],
                            lhsT=gcodes[:, t, m0 : m0 + 128].bitcast(FP8X4),
                            lhsT_scale=gsc[:, t, m0 : m0 + 128],
                            rhs=xcodes[n][:, g, 512 * h : 512 * h + 512].bitcast(FP8X4),
                            rhs_scale=xsc[n][:, g, 512 * h : 512 * h + 512],
                            start=(g == 0),
                            stop=(g == 1),
                        )

        def rsq(k):
            t = k % 4
            otile[k] = opool.tile([P, 2 * HW], F32, name="o")
            for e1 in range(2):
                for h in range(2):
                    c0 = HW * e1 + 512 * h
                    cuts = 2 if (k, e1, h) == (NSLOT - 1, 1, 1) else 1
                    wd = 512 // cuts
                    for q in range(cuts):
                        nc.scalar.activation(
                            out=otile[k][:, c0 + q * wd : c0 + (q + 1) * wd],
                            in_=acc[(k, e1, h)][:, q * wd : (q + 1) * wd],
                            func=ACT.Abs_reciprocal_sqrt,
                            bias=beff[:, 2 * t + e1 : 2 * t + e1 + 1],
                            scale=1.0,
                        )

        def finish(k, c0, c1):
            n, t = k // 4, k % 4
            r0 = 2 * (t % 2)
            cols = slice(c0, c1)
            if (n, t // 2) == (0, 0):
                o3 = otile[k][:].rearrange("p (e w) -> p e w", e=2)
                for q in range(3):
                    w0, wd = first_parts[q]
                    nc.vector.tensor_tensor(
                        out=o3[:, :, w0 : w0 + wd], in0=o3[:, :, w0 : w0 + wd],
                        in1=xfirst[q][:, r0 : r0 + 2, :], op=ALU.mult,
                    )
            else:
                xrow = xs[(n, t // 2)][:, r0 : r0 + 2, :].rearrange("p e w -> p (e w)")
                nc.vector.tensor_tensor(
                    out=otile[k][:, cols], in0=otile[k][:, cols], in1=xrow[:, cols], op=ALU.mult
                )
            nc.sync.dma_start(out=out_v[n, t][:, cols], in_=otile[k][:, cols])

        g_relu((0, 0))
        g_transpose(0, 0)
        sq_scalar(0)
        g_relu((0, 1))
        g_transpose(0, 1)
        g_square(0, 0)
        g_square(0, 1)
        sq_quant(0)
        sq_vector(1)
        g_relu(1)
        g_transpose(1, 0)
        g_transpose(1, 1)
        sq_vector(2)
        sq_scalar(2)
        g_sub(0, 0)
        g_relu(2)
        g_transpose(2, 0)
        g_transpose(2, 1)
        g_sub(0, 1)
        g_square(1, 0)
        g_square(1, 1)
        g_relu(3)
        g_transpose(3, 0)
        g_transpose(3, 1)
        sq_quant(1)
        g_quant(0)
        sq_quant(2)
        g_sub(1, 0)
        g_sub(1, 1)
        g_square(2, 0)
        g_square(2, 1)
        sq_vector(3)
        g_quant(1)
        g_sub(2, 0)
        g_sub(2, 1)
        g_square(3, 0)
        g_square(3, 1)
        sq_vector(4)
        g_quant(2)
        sq_scalar(3)
        sq_scalar(4)
        g_sub(3, 0)
        g_sub(3, 1)
        sq_quant(3)

        bmax = const.tile([P, 8], F32, name="bmax")
        beff = const.tile([P, 8], F32, name="beff")
        nc.vector.tensor_scalar(
            out=bmax[:], in0=bt[:].rearrange("p t e -> p (t e)"),
            scalar1=BOUND_BETA, scalar2=None, op0=ALU.max,
        )
        nc.vector.tensor_tensor(out=beff[:], in0=bmax[:], in1=bmax[:], op=ALU.mult)
        nc.vector.tensor_scalar(
            out=beff[:], in0=beff[:], scalar1=-PEDESTAL, scalar2=None, op0=ALU.add
        )
        g_quant(3)
        sq_quant(4)

        vnext = 5
        qnext = 5
        for j in range(5, LEAD):
            sq_scalar(j)
            while vnext <= j + 1:
                sq_vector(vnext)
                vnext += 1
            if qnext < j:
                sq_quant(qnext)
                qnext += 1

        for k in range(NSLOT):
            j = k + LEAD
            if j < npiece:
                sq_scalar(j)
            mm(k)
            rsq(k)
            if k >= 1:
                finish(k - 1, HW if k - 1 >= HALVES_FROM else 0, 2 * HW)
            while vnext <= j + 1 and vnext < npiece:
                sq_vector(vnext)
                vnext += 1
            if qnext < npiece:
                sq_quant(qnext)
                qnext += 1
            if HALVES_FROM <= k < NSLOT - 1:
                finish(k, 0, HW)
        for c0, c1 in ((0, 512), (512, 1024), (1024, 1536), (1536, 1792), (1792, 2048)):
            finish(NSLOT - 1, c0, c1)
